import numpy as np
import ml_dtypes


def mxq(x, axis, fmt="e4m3"):
    dtype, down = {"e4m3": (ml_dtypes.float8_e4m3fn, 7), "e5m2": (ml_dtypes.float8_e5m2, 14)}[fmt]
    v = np.moveaxis(np.asarray(x, np.float32).astype(ml_dtypes.bfloat16).astype(np.float64), axis, -1)
    blocks = v.reshape(v.shape[:-1] + (-1, 32))
    amax = np.abs(blocks).max(-1, keepdims=True)
    byte = np.maximum(np.where(amax > 0, np.frexp(amax)[1] - 1 + 127, 0) - down, 1)
    scale = np.exp2(byte - 127.0)
    codes = (blocks / scale).astype(np.float32).astype(dtype).astype(np.float64)
    return np.moveaxis((codes * scale).reshape(v.shape), -1, axis)


WIDE = False


def mx_kscale(k):
    if not WIDE:
        return np.ones(k)
    levels = np.array([10, -10, 5, -5, 0])
    if k % 512:
        return np.exp2(np.random.permutation(np.resize(levels, k // 32))).repeat(32)
    a = np.empty((k // 512, 16))
    for p in range(k // 512):
        a[p, :8] = np.random.permutation(np.resize(levels, 8))
        for g in range(8):
            far = levels[np.abs(levels - a[p, g]) >= 10]
            a[p, g + 8] = far[np.random.randint(len(far))]
    return np.exp2(a.ravel()).repeat(32)


BF16 = ml_dtypes.bfloat16


def bf(x):
    return np.asarray(x, np.float32).astype(BF16)


def f64(x):
    return np.asarray(x).astype(np.float64)


B, T, D, M, C = 1, 2048, 2048, 4, 1024
MD = M * D
LN_EPS = 1e-5


def setup_inputs():
    s, t = mx_kscale(T), mx_kscale(MD)
    sc = np.random.standard_normal((B, M, T, T)) * 2.0
    sc = np.where(np.tril(np.ones((T, T), dtype=bool)), sc, -np.inf)
    e = np.exp(sc - sc.max(-1, keepdims=True))
    attn = e / e.sum(-1, keepdims=True)
    return {"attn": bf(attn * s),
            "pz": bf(np.random.standard_normal((B, M, T, D)) / s[:, None] * t.reshape(M, 1, D)),
            "Wo": bf(np.random.standard_normal((D, MD)) * 2.0 / np.sqrt(MD) / t),
            "bo": bf(np.random.standard_normal(D) * 0.3),
            "x": bf(np.random.standard_normal((B, T, D))),
            "gamma": bf(1.0 + 0.1 * np.random.standard_normal(D)),
            "beta": bf(0.1 * np.random.standard_normal(D))}


def reference(attn, pz, Wo, bo, x, gamma, beta):
    a = f64(attn)
    pq = mxq(f64(pz), 2, "e4m3")
    rows = []
    for r in range(0, T, C):
        aq = mxq(a[:, :, r:r + C, :r + C], 3, "e4m3")
        rows.append(aq @ pq[:, :, :r + C, :])
    out = np.concatenate(rows, axis=2)
    cat = out.transpose(0, 2, 1, 3).reshape(B, T, MD)
    y = (mxq(cat, 2, "e4m3") @ mxq(f64(Wo), 1, "e4m3").T) + f64(bo)
    h = y + f64(x)
    mu = h.mean(-1, keepdims=True)
    var = h.var(-1, keepdims=True)
    return (h - mu) / np.sqrt(var + LN_EPS) * f64(gamma) + f64(beta)

@@ -1,0 +1,403 @@
+from contextlib import ExitStack
+
+import concourse.mybir as mybir
+from concourse.masks import make_identity
+
+F32 = mybir.dt.float32
+BF16 = mybir.dt.bfloat16
+U32 = mybir.dt.uint32
+U8 = mybir.dt.uint8
+FP8X4 = mybir.dt.float8_e4m3fn_x4
+ALU = mybir.AluOpType
+ACT = mybir.ActivationFunctionType
+AX = mybir.AxisListType
+
+P = 128
+T = 2048
+D = 2048
+H = 4
+MD = H * D
+EPS = 1e-5
+FLOPS = 2 * H * D * (1024 * 1024 + 1024 * 2048) + 2 * T * MD * D
+
+NCODE = 28
+NRAW = 4
+NGRP = 3
+NPLANE = 9
+NHALF = 8
+NF1K = 4
+NSINGLE = 5
+NOC = 8
+NSTEP = 2 + 64 + 128
+
+
+def tile_softmaxattention_pb_l_kernel(tc, attn, pz, Wo, bo, x, gamma, beta, out):
+    nc = tc.nc
+
+    jobs = [(oc, tt) for oc in range(NSINGLE) for tt in range(16)]
+    jobs += [(oc, tt) for tt in range(16) for oc in range(NSINGLE, NOC)]
+    first_job = {}
+    last_job = {}
+    for j, (oc, tt) in enumerate(jobs):
+        if oc not in first_job:
+            first_job[oc] = j
+        last_job[oc] = j
+
+    t_at = [[] for st in range(NSTEP)]
+    mand = [0] * NSTEP
+    for m in range(H):
+        units = [(tc_, g) for tc_ in range(4) for g in range(tc_ + 1)]
+        for i, (tc_, g) in enumerate(units):
+            if m == 0:
+                st = 1 + tc_
+            elif m == 1:
+                st = 2 + 3 + (i * 13) // 10
+            else:
+                st = 2 + 16 * (m - 1) + (i * 16) // 10
+            t_at[st].append(("a", m, tc_, g))
+            for z in range(st, 2 + 16 * m + 12 + tc_ + 1):
+                mand[z] += 1
+    for q in range(64):
+        for z in range(q + 1, 2 + 4 * (q // 4) + 3 + 1):
+            mand[z] += 1
+    gb_step = 66 + first_job[NSINGLE - 1]
+    for z in range(gb_step, NSTEP):
+        mand[z] += 4
+    st = 2 + 48
+    for w in range(NOC * 8):
+        oc = w // 8
+        end = 66 + last_job[oc]
+        while True:
+            ok = len(t_at[st]) < (1 if st < 66 + first_job[NSINGLE] else 3)
+            if ok:
+                ok = all(mand[z] + 1 <= NCODE for z in range(st, end + 1))
+            if ok:
+                break
+            st += 1
+        assert st <= 66 + first_job[oc], "a Wo unit comes too late"
+        t_at[st].append(("w", oc, w % 8))
+        for z in range(st, end + 1):
+            mand[z] += 1
+
+    last_t_step = max(z for z in range(NSTEP) if t_at[z])
+
+    raw_order = []
+    for st in range(NSTEP):
+        q = st
+        if q < 64:
+            raw_order.append(("p", q // 16, (q % 16) // 4, q % 4))
+        raw_order.extend(t_at[st])
+
+    with ExitStack() as ctx:
+        ctx.enter_context(tc.manual_schedule())
+        sb = ctx.enter_context(tc.tile_pool(name="sb", bufs=1))
+        ps = ctx.enter_context(tc.psum_pool(name="ps", bufs=8))
+
+        ident = sb.tile([P, P], F32, name="ident")
+        make_identity(nc, ident[:])
+        neg_half = sb.tile([P, 1], F32, name="neg_half")
+        nc.vector.memset(neg_half[:], -0.5)
+        warm = sb.tile([P, 1], F32, name="warm")
+        nc.scalar.activation(out=warm[:], in_=neg_half[:], func=ACT.Square)
+        sums = sb.tile([P, 16, 2, NOC], F32, name="sums")
+
+        cat_code = [sb.tile([P, T], U32, name="cat%d" % g, align_bytes=64) for g in range(16)]
+        cat_plane = [sb.tile([P, T], U8, name="catp%d" % i, align_bytes=64) for i in range(4)]
+
+        def new_code():
+            return sb.tile([P, 512], U32, name="code", tag="code", bufs=NCODE, align_bytes=64)
+
+        def new_plane():
+            return sb.tile([P, 512], U8, name="plane", tag="plane", bufs=NPLANE, align_bytes=64)
+
+        def new_grp():
+            return sb.tile([P, 2048], BF16, name="grp", tag="grp", bufs=NGRP, align_bytes=64)
+
+        def new_bank():
+            return ps.tile([P, 512], F32, name="bank", tag="bank")
+
+        raws = {}
+        issued = [0]
+
+        rows = {}
+        raw_cap = [NRAW]
+
+        def issue_raw():
+            while issued[0] < len(raw_order) and len(raws) < raw_cap[0] and len(raws) + len(rows) < NRAW:
+                issue_one_raw()
+
+        def issue_one_raw():
+            u = raw_order[issued[0]]
+            issued[0] += 1
+            raw = sb.tile([P, 2048], BF16, name="raw", tag="raw", bufs=NRAW, align_bytes=64)
+            if u[0] == "p":
+                m, ib, g = u[1], u[2], u[3]
+                nc.sync.dma_start(
+                    out=raw[:].rearrange("p (j c) -> p j c", j=4),
+                    in_=pz[0, m, 512 * g:512 * (g + 1), 512 * ib:512 * (ib + 1)].rearrange("(p j) c -> p j c", j=4),
+                )
+            elif u[0] == "a":
+                m, tc_, g = u[1], u[2], u[3]
+                nc.sync.dma_start(
+                    out=raw[:].rearrange("p (a k) -> p a k", a=4),
+                    in_=attn[0, m, 512 * tc_:512 * (tc_ + 1), 512 * g:512 * (g + 1)].rearrange("(a p) k -> p a k", p=P),
+                )
+            else:
+                oc, gp = u[1], u[2]
+                nc.sync.dma_start(
+                    out=raw[:].rearrange("p (a k) -> p a k", a=2),
+                    in_=Wo[256 * oc:256 * (oc + 1), 1024 * gp:1024 * (gp + 1)].rearrange("(a p) k -> p a k", p=P),
+                )
+            raws[u] = raw
+
+        issue_raw()
+
+        t_code = {}
+        t_plane = {}
+        pending = []
+
+        def t_quantize():
+            while pending:
+                u, grp = pending.pop(0)
+                if u[0] == "a":
+                    pkey, k = ("a", u[1], u[2]), 4 * u[3]
+                else:
+                    pkey, k = ("w", u[1], u[2] // 4), 4 * (u[2] % 4)
+                if pkey not in t_plane:
+                    t_plane[pkey] = new_plane()
+                code = new_code()
+                nc.vector.quantize_mx(out=code[:].bitcast(FP8X4), scales=t_plane[pkey][k:P, :], in_=grp[:])
+                t_code[u] = code
+
+        def t_transpose(u):
+            raw32 = raws.pop(u)[:].bitcast(F32)
+            if u[0] == "a":
+                bases = [0, 256, 512, 768]
+            else:
+                bases = [0, 512, 256, 768]
+            banks = []
+            for b in range(2):
+                bank = new_bank()
+                for c in range(2):
+                    base = bases[2 * b + c]
+                    for w in range(2):
+                        col = (2 * c + w) * P
+                        nc.tensor.transpose(bank[:, col:col + P], raw32[:, base + w:base + 256:2], ident[:])
+                banks.append(bank)
+            issue_raw()
+            t_quantize()
+            grp = new_grp()
+            g32 = grp[:].bitcast(F32)
+            for b in range(2):
+                nc.scalar.copy(
+                    out=g32[:, 512 * b:512 * (b + 1)].rearrange("p (c r w) -> p c r w", c=2, w=2),
+                    in_=banks[b][:].rearrange("p (c w r) -> p c r w", c=2, w=2),
+                )
+            pending.append((u, grp))
+
+        p_grp = {}
+        p_code = {}
+        p_plane = {}
+
+        def p_interleave(q):
+            u = ("p", q // 16, (q % 16) // 4, q % 4)
+            raw = raws.pop(u)
+            grp = new_grp()
+            nc.vector.tensor_copy(
+                out=grp[:].rearrange("p (t m j) -> p t m j", t=4, j=4),
+                in_=raw[:].rearrange("p (j m t) -> p t m j", j=4, t=4),
+            )
+            issue_raw()
+            p_grp[q] = grp
+
+        def p_quantize(q):
+            code = new_code()
+            plane = sb.tile([P, 512], U8, name="pplane", tag="half", bufs=NHALF, align_bytes=64)
+            nc.vector.quantize_mx(out=code[:].bitcast(FP8X4), scales=plane[:], in_=p_grp.pop(q)[:])
+            p_code[q] = code
+            p_plane[q] = plane
+
+        c_grp = {}
+
+        def c_matmuls(s):
+            m, ib, tc_ = s // 16, (s % 16) // 4, s % 4
+            grp = new_grp()
+            for tq in range(4):
+                bank = new_bank()
+                for t4 in range(4):
+                    for g in range(tc_ + 1):
+                        q = 16 * m + 4 * ib + g
+                        a = ("a", m, tc_, g)
+                        nc.tensor.matmul_mx(
+                            out=bank[:, P * t4:P * (t4 + 1)],
+                            lhsT=p_code[q][:, P * t4:P * (t4 + 1)].bitcast(FP8X4),
+                            lhsT_scale=p_plane[q][:, P * t4:P * (t4 + 1)],
+                            rhs=t_code[a][:, P * tq:P * (tq + 1)].bitcast(FP8X4),
+                            rhs_scale=t_plane[("a", m, tc_)][4 * g:P, P * tq:P * (tq + 1)],
+                            start=(g == 0),
+                            stop=(g == tc_),
+                        )
+                nc.scalar.copy(
+                    out=grp[:, 512 * tq:512 * (tq + 1)].rearrange("p (r j) -> p r j", j=4),
+                    in_=bank[:].rearrange("p (j r) -> p r j", j=4),
+                )
+            c_grp[s] = grp
+
+        def cat_slot(g):
+            return cat_plane[(g // 8) * 2 + g % 2], 4 * ((g // 2) % 4)
+
+        def c_quantize(s):
+            m, ib, tc_ = s // 16, (s % 16) // 4, s % 4
+            g = 4 * m + ib
+            plane, k = cat_slot(g)
+            nc.vector.quantize_mx(
+                out=cat_code[g][:, 512 * tc_:512 * (tc_ + 1)].bitcast(FP8X4),
+                scales=plane[k:P, 512 * tc_:512 * (tc_ + 1)],
+                in_=c_grp.pop(s)[:],
+            )
+
+        for st in range(66):
+            s = st - 2
+            if 0 <= s + 1 < 64:
+                p_quantize(s + 1)
+            if s + 2 < 64:
+                p_interleave(s + 2)
+            t_quantize()
+            for u in t_at[st]:
+                t_transpose(u)
+            if s >= 1:
+                c_quantize(s - 1)
+            if s >= 0:
+                c_matmuls(s)
+
+        xts = {}
+        xbs = {}
+        bobs = {}
+        gb = {}
+        parked = []
+        next_rows = [0]
+
+        def load_bo(oc):
+            bob = sb.tile([P, 256], BF16, name="bob", tag="half", bufs=NHALF, align_bytes=64)
+            nc.sync.dma_start(out=bob[:], in_=bo[256 * oc:256 * (oc + 1)].partition_broadcast(P))
+            bobs[oc] = bob
+
+        def load_x(j):
+            if j >= len(jobs):
+                return
+            oc, tt = jobs[j]
+            xt = sb.tile([P, 256], BF16, name="xt", tag="half", bufs=NHALF, align_bytes=64)
+            nc.sync.dma_start(out=xt[:], in_=x[0, P * tt:P * (tt + 1), 256 * oc:256 * (oc + 1)])
+            xts[j] = xt
+
+        def add_bias(j):
+            if j >= len(jobs):
+                return
+            oc, tt = jobs[j]
+            xb = sb.tile([P, 256], F32, name="xb", tag="f1k", bufs=NF1K, align_bytes=64)
+            nc.gpsimd.tensor_tensor(out=xb[:], in0=xts.pop(j)[:], in1=bobs[oc][:], op=ALU.add)
+            xbs[j] = xb
+
+        def load_rows(upto):
+            while next_rows[0] <= min(upto, 15) and len(raws) + len(rows) < NRAW and len(rows) < NGRP:
+                load_rows_of(next_rows[0])
+                next_rows[0] += 1
+
+        def load_rows_of(tt):
+            ha = sb.tile([P, 1024], F32, name="ha", tag="raw", bufs=NRAW, align_bytes=64)
+            hb = sb.tile([P, 1024], F32, name="hb", tag="grp", bufs=NGRP, align_bytes=64)
+            nc.sync.dma_start(out=ha[:], in_=out[0, P * tt:P * (tt + 1), 0:1024])
+            npark = 256 * NSINGLE - 1024
+            nc.sync.dma_start(out=hb[:, 0:npark], in_=out[0, P * tt:P * (tt + 1), 1024:1024 + npark])
+            rows[tt] = (ha, hb)
+
+        def y_matmuls(j):
+            oc, tt = jobs[j]
+            bank = new_bank()
+            for g in range(16):
+                gp, gg = g // 2, g % 2
+                plane, k = cat_slot(g)
+                nc.tensor.matmul_mx(
+                    out=bank[:, 0:256],
+                    lhsT=cat_code[g][:, P * tt:P * (tt + 1)].bitcast(FP8X4),
+                    lhsT_scale=plane[k:P, P * tt:P * (tt + 1)],
+                    rhs=t_code[("w", oc, gp)][:, 256 * gg:256 * (gg + 1)].bitcast(FP8X4),
+                    rhs_scale=t_plane[("w", oc, gp // 4)][k:P, 256 * gg:256 * (gg + 1)],
+                    start=(g == 0),
+                    stop=(g == 15),
+                )
+            if oc < NSINGLE:
+                h = sb.tile([P, 256], F32, name="h", tag="f1k", bufs=NF1K, align_bytes=64)
+                hv = h[:]
+                parked.append((oc, tt, h))
+            else:
+                hv = rows[tt][1][:, 256 * (oc - 4):256 * (oc - 3)]
+            nc.vector.tensor_tensor(out=hv, in0=bank[:, 0:256], in1=xbs.pop(j)[:], op=ALU.add)
+            junk = sb.tile([P, 256], BF16, name="junk", tag="junk", bufs=1, align_bytes=64)
+            nc.scalar.activation(out=junk[:], in_=hv, func=ACT.Identity, scale=1.0 / D, accum_out=sums[:, tt, 0, oc:oc + 1])
+            nc.scalar.activation(out=junk[:], in_=hv, func=ACT.Square, scale=D ** -0.5, accum_out=sums[:, tt, 1, oc:oc + 1])
+
+        def park():
+            while parked:
+                oc, tt, h = parked.pop(0)
+                nc.sync.dma_start(out=out[0, P * tt:P * (tt + 1), 256 * oc:256 * (oc + 1)], in_=h[:])
+
+        def finalize(tt):
+            ha, hb = rows.pop(tt)
+            st4 = sb.tile([P, 4], F32, name="st4", tag="st4", bufs=2)
+            rstd = sb.tile([P, 1], F32, name="rstd", tag="rstd", bufs=2)
+            nc.vector.tensor_reduce(out=st4[:, 0:2], in_=sums[:, tt, :, :], axis=AX.X, op=ALU.add)
+            nc.vector.tensor_scalar(out=st4[:, 2:3], in0=st4[:, 0:1], scalar1=st4[:, 0:1], scalar2=EPS, op0=ALU.mult, op1=ALU.subtract)
+            nc.vector.tensor_tensor(out=st4[:, 3:4], in0=st4[:, 1:2], in1=st4[:, 2:3], op=ALU.subtract)
+            nc.gpsimd.tensor_tensor(out=rstd[:], in0=st4[:, 3:4], in1=neg_half[:], op=ALU.pow)
+            for i, hx in enumerate((ha, hb)):
+                nc.vector.scalar_tensor_tensor(out=hx[:], in0=hx[:], scalar=st4[:, 0:1], in1=gb[("g", i)][:], op0=ALU.subtract, op1=ALU.mult)
+            for i, hx in enumerate((ha, hb)):
+                nc.vector.scalar_tensor_tensor(out=hx[:], in0=hx[:], scalar=rstd[:], in1=gb[("b", i)][:], op0=ALU.mult, op1=ALU.add)
+                nc.scalar.dma_start(out=out[0, P * tt:P * (tt + 1), 1024 * i:1024 * (i + 1)], in_=hx[:])
+
+        load_bo(0)
+        for j in range(3):
+            load_x(j)
+        add_bias(0)
+        to_finalize = []
+        for j in range(len(jobs)):
+            st = 66 + j
+            oc, tt = jobs[j]
+            t_quantize()
+            for u in t_at[st]:
+                t_transpose(u)
+            if any(("w", oc, gp) not in t_code for gp in range(8)):
+                t_quantize()
+            if j == 0:
+                c_quantize(63)
+            if st == gb_step:
+                for i in range(2):
+                    for nm, src in (("g", gamma), ("b", beta)):
+                        t = sb.tile([P, 1024], BF16, name="gb", tag="code", bufs=NCODE, align_bytes=64)
+                        nc.sync.dma_start(out=t[:], in_=src[1024 * i:1024 * (i + 1)].partition_broadcast(P))
+                        gb[(nm, i)] = t
+            if j + 1 < len(jobs) and jobs[j + 1][0] not in bobs:
+                load_bo(jobs[j + 1][0])
+            if j + 2 < len(jobs) and jobs[j + 2][0] not in bobs:
+                load_bo(jobs[j + 2][0])
+            load_x(j + 3)
+            add_bias(j + 1)
+            if j + 4 >= first_job[NSINGLE]:
+                raw_cap[0] = NRAW - 1
+            if oc >= NSINGLE:
+                load_rows(tt + 1 if st > last_t_step else tt)
+            y_matmuls(j)
+            if oc < NSINGLE:
+                if len(parked) > 1:
+                    oc0, tt0, h0 = parked.pop(0)
+                    nc.sync.dma_start(out=out[0, P * tt0:P * (tt0 + 1), 256 * oc0:256 * (oc0 + 1)], in_=h0[:])
+            else:
+                park()
+                if oc == NSINGLE:
+                    while to_finalize:
+                        finalize(to_finalize.pop(0))
+                if oc == NOC - 1:
+                    to_finalize.append(tt)
+        while to_finalize:
+            finalize(to_finalize.pop(0))

@@ -20,12 +20,13 @@ MD = H * D
 EPS = 1e-5
 FLOPS = 2 * H * D * (1024 * 1024 + 1024 * 2048) + 2 * T * MD * D
 
-NCODE = 28
+NCODE = 25
 NRAW = 4
 NGRP = 3
-NPLANE = 9
-NHALF = 8
-NF1K = 4
+NPLANE = 8
+NHALF = 9
+NF1K = 5
+NSRT = 2
 NSINGLE = 5
 NOC = 8
 NSTEP = 2 + 64 + 128
@@ -60,15 +61,17 @@ def tile_softmaxattention_pb_l_kernel(tc, attn, pz, Wo, bo, x, gamma, beta, out)
     for q in range(64):
         for z in range(q + 1, 2 + 4 * (q // 4) + 3 + 1):
             mand[z] += 1
-    gb_step = 66 + first_job[NSINGLE - 1]
-    for z in range(gb_step, NSTEP):
-        mand[z] += 4
     st = 2 + 48
     for w in range(NOC * 8):
         oc = w // 8
         end = 66 + last_job[oc]
         while True:
-            ok = len(t_at[st]) < (1 if st < 66 + first_job[NSINGLE] else 3)
+            if st < 66:
+                ok = len(t_at[st]) < 1 and ((st - 50) * 10) // 16 != ((st - 49) * 10) // 16
+            elif st < 66 + first_job[NSINGLE]:
+                ok = len(t_at[st]) < 2 and (st % 2 == 0)
+            else:
+                ok = len(t_at[st]) < 3
             if ok:
                 ok = all(mand[z] + 1 <= NCODE for z in range(st, end + 1))
             if ok:
@@ -81,12 +84,25 @@ def tile_softmaxattention_pb_l_kernel(tc, attn, pz, Wo, bo, x, gamma, beta, out)
 
     last_t_step = max(z for z in range(NSTEP) if t_at[z])
 
+    sort_at = [[] for st in range(NSTEP)]
+    presorted = set()
+    live = 0
+    for st in range(NSTEP):
+        live -= len([u for u in t_at[st] if u in presorted])
+        for d in (1, 2):
+            for u in t_at[min(st + d, NSTEP - 1)]:
+                if u not in presorted and u[0:2] != ("a", 0) and live < NSRT and st + d < NSTEP:
+                    sort_at[st].append(u)
+                    presorted.add(u)
+                    live += 1
+
     raw_order = []
     for st in range(NSTEP):
         q = st
         if q < 64:
             raw_order.append(("p", q // 16, (q % 16) // 4, q % 4))
-        raw_order.extend(t_at[st])
+        raw_order.extend(u for u in t_at[st] if u not in presorted)
+        raw_order.extend(sort_at[st])
 
     with ExitStack() as ctx:
         ctx.enter_context(tc.manual_schedule())
@@ -120,10 +136,11 @@ def tile_softmaxattention_pb_l_kernel(tc, attn, pz, Wo, bo, x, gamma, beta, out)
         issued = [0]
 
         rows = {}
+        rows_a = {}
         raw_cap = [NRAW]
 
         def issue_raw():
-            while issued[0] < len(raw_order) and len(raws) < raw_cap[0] and len(raws) + len(rows) < NRAW:
+            while issued[0] < len(raw_order) and len(raws) < raw_cap[0] and len(raws) + len(rows_a) + len([z for z in rows if z % 5 >= 3]) < NRAW:
                 issue_one_raw()
 
         def issue_one_raw():
@@ -169,8 +186,29 @@ def tile_softmaxattention_pb_l_kernel(tc, attn, pz, Wo, bo, x, gamma, beta, out)
                 nc.vector.quantize_mx(out=code[:].bitcast(FP8X4), scales=t_plane[pkey][k:P, :], in_=grp[:])
                 t_code[u] = code
 
-        def t_transpose(u):
+        sorted_words = {}
+        n_sorted = [0]
+
+        def t_sort(u):
             raw32 = raws.pop(u)[:].bitcast(F32)
+            srt = sb.tile([P, 1024], F32, name="srt", tag="srt", bufs=NSRT, align_bytes=64)
+            n_sorted[0] += 1
+            if u[0] == "w" or n_sorted[0] % 2 == 0:
+                eng = nc.vector.tensor_copy
+            else:
+                eng = nc.scalar.copy
+            eng(
+                out=srt[:].rearrange("p (c w k) -> p c w k", c=4, w=2),
+                in_=raw32.rearrange("p (c k w) -> p c w k", c=4, w=2),
+            )
+            issue_raw()
+            sorted_words[u] = srt
+
+        def t_transpose(u):
+            if u in sorted_words:
+                words, step = sorted_words.pop(u), 1
+            else:
+                words, step = raws.pop(u)[:].bitcast(F32), 2
             if u[0] == "a":
                 bases = [0, 256, 512, 768]
             else:
@@ -182,7 +220,10 @@ def tile_softmaxattention_pb_l_kernel(tc, attn, pz, Wo, bo, x, gamma, beta, out)
                     base = bases[2 * b + c]
                     for w in range(2):
                         col = (2 * c + w) * P
-                        nc.tensor.transpose(bank[:, col:col + P], raw32[:, base + w:base + 256:2], ident[:])
+                        if step == 1:
+                            nc.tensor.transpose(bank[:, col:col + P], words[:, base + P * w:base + P * (w + 1)], ident[:])
+                        else:
+                            nc.tensor.transpose(bank[:, col:col + P], words[:, base + w:base + 256:2], ident[:])
                 banks.append(bank)
             issue_raw()
             t_quantize()
@@ -265,51 +306,81 @@ def tile_softmaxattention_pb_l_kernel(tc, attn, pz, Wo, bo, x, gamma, beta, out)
             t_quantize()
             for u in t_at[st]:
                 t_transpose(u)
+            for u in sort_at[st]:
+                t_sort(u)
             if s >= 1:
                 c_quantize(s - 1)
             if s >= 0:
                 c_matmuls(s)
 
         xts = {}
-        xbs = {}
+        hdst = {}
         bobs = {}
         gb = {}
         parked = []
         next_rows = [0]
+        next_a = [0]
+        next_x = [0]
+        next_bias = [0]
+        junk = sb.tile([P, 256], BF16, name="junk", align_bytes=64)
 
-        def load_bo(oc):
-            bob = sb.tile([P, 256], BF16, name="bob", tag="half", bufs=NHALF, align_bytes=64)
-            nc.sync.dma_start(out=bob[:], in_=bo[256 * oc:256 * (oc + 1)].partition_broadcast(P))
-            bobs[oc] = bob
+        n_single = 16 * NSINGLE
+        late = [(oc, tt) for tt in range(16) for oc in range(NSINGLE, NOC)]
+        xlist = []
+        x_pos = {}
+        for j in range(n_single):
+            x_pos[j] = len(xlist)
+            xlist.append((jobs[j][0], jobs[j][1], j))
+            for i in range((j * len(late)) // (n_single - 8), min(len(late), ((j + 1) * len(late)) // (n_single - 8))):
+                xlist.append((late[i][0], late[i][1], -1))
 
-        def load_x(j):
-            if j >= len(jobs):
-                return
-            oc, tt = jobs[j]
-            xt = sb.tile([P, 256], BF16, name="xt", tag="half", bufs=NHALF, align_bytes=64)
-            nc.sync.dma_start(out=xt[:], in_=x[0, P * tt:P * (tt + 1), 256 * oc:256 * (oc + 1)])
-            xts[j] = xt
+        def load_x(upto):
+            while next_x[0] <= min(upto, len(xlist) - 1):
+                j = next_x[0]
+                next_x[0] += 1
+                oc, tt = xlist[j][0], xlist[j][1]
+                if oc not in bobs:
+                    bob = sb.tile([P, 256], BF16, name="bob", tag="half", bufs=NHALF, align_bytes=64)
+                    nc.sync.dma_start(out=bob[:], in_=bo[256 * oc:256 * (oc + 1)].partition_broadcast(P))
+                    bobs[oc] = bob
+                xt = sb.tile([P, 256], BF16, name="xt", tag="half", bufs=NHALF, align_bytes=64)
+                nc.sync.dma_start(out=xt[:], in_=x[0, P * tt:P * (tt + 1), 256 * oc:256 * (oc + 1)])
+                xts[j] = xt
 
-        def add_bias(j):
-            if j >= len(jobs):
-                return
-            oc, tt = jobs[j]
-            xb = sb.tile([P, 256], F32, name="xb", tag="f1k", bufs=NF1K, align_bytes=64)
-            nc.gpsimd.tensor_tensor(out=xb[:], in0=xts.pop(j)[:], in1=bobs[oc][:], op=ALU.add)
-            xbs[j] = xb
-
-        def load_rows(upto):
-            while next_rows[0] <= min(upto, 15) and len(raws) + len(rows) < NRAW and len(rows) < NGRP:
-                load_rows_of(next_rows[0])
+        def load_hb(upto):
+            while next_rows[0] <= min(upto, 15):
+                tt = next_rows[0]
+                if tt % 5 < 3:
+                    if len(pending) + len([z for z in rows if z % 5 < 3]) >= NGRP:
+                        return
+                    hb = sb.tile([P, 1024], F32, name="hb", tag="grp", bufs=NGRP, align_bytes=64)
+                else:
+                    if len(raws) + len(rows_a) + len([z for z in rows if z % 5 >= 3]) >= NRAW:
+                        return
+                    hb = sb.tile([P, 1024], F32, name="hb", tag="raw", bufs=NRAW, align_bytes=64)
                 next_rows[0] += 1
+                nc.sync.dma_start(out=hb[:], in_=out[0, P * tt:P * (tt + 1), 1024:2048])
+                rows[tt] = hb
 
-        def load_rows_of(tt):
-            ha = sb.tile([P, 1024], F32, name="ha", tag="raw", bufs=NRAW, align_bytes=64)
-            hb = sb.tile([P, 1024], F32, name="hb", tag="grp", bufs=NGRP, align_bytes=64)
-            nc.sync.dma_start(out=ha[:], in_=out[0, P * tt:P * (tt + 1), 0:1024])
-            npark = 256 * NSINGLE - 1024
-            nc.sync.dma_start(out=hb[:, 0:npark], in_=out[0, P * tt:P * (tt + 1), 1024:1024 + npark])
-            rows[tt] = (ha, hb)
+        def load_ha(upto):
+            while next_a[0] <= min(upto, 15) and len(rows_a) < 2 and len(raws) + len(rows_a) + len([z for z in rows if z % 5 >= 3]) < NRAW:
+                tt = next_a[0]
+                next_a[0] += 1
+                ha = sb.tile([P, 1024], F32, name="ha", tag="raw", bufs=NRAW, align_bytes=64)
+                nc.sync.dma_start(out=ha[:], in_=out[0, P * tt:P * (tt + 1), 0:1024])
+                rows_a[tt] = ha
+
+        def add_bias(upto):
+            while next_bias[0] <= min(upto, len(xlist) - 1):
+                i = next_bias[0]
+                next_bias[0] += 1
+                oc, tt, j = xlist[i]
+                h = sb.tile([P, 256], F32, name="h", tag="f1k", bufs=NF1K, align_bytes=64)
+                nc.gpsimd.tensor_tensor(out=h[:], in0=xts.pop(i)[:], in1=bobs[oc][:], op=ALU.add)
+                if j >= 0:
+                    hdst[j] = h[:]
+                else:
+                    parked.append((oc, tt, h[:]))
 
         def y_matmuls(j):
             oc, tt = jobs[j]
@@ -327,39 +398,36 @@ def tile_softmaxattention_pb_l_kernel(tc, attn, pz, Wo, bo, x, gamma, beta, out)
                     stop=(g == 15),
                 )
             if oc < NSINGLE:
-                h = sb.tile([P, 256], F32, name="h", tag="f1k", bufs=NF1K, align_bytes=64)
-                hv = h[:]
-                parked.append((oc, tt, h))
+                hv = hdst.pop(j)
             else:
-                hv = rows[tt][1][:, 256 * (oc - 4):256 * (oc - 3)]
-            nc.vector.tensor_tensor(out=hv, in0=bank[:, 0:256], in1=xbs.pop(j)[:], op=ALU.add)
-            junk = sb.tile([P, 256], BF16, name="junk", tag="junk", bufs=1, align_bytes=64)
+                hv = rows[tt][:, 256 * (oc - 4):256 * (oc - 3)]
+            nc.vector.tensor_tensor(out=hv, in0=bank[:, 0:256], in1=hv, op=ALU.add)
             nc.scalar.activation(out=junk[:], in_=hv, func=ACT.Identity, scale=1.0 / D, accum_out=sums[:, tt, 0, oc:oc + 1])
             nc.scalar.activation(out=junk[:], in_=hv, func=ACT.Square, scale=D ** -0.5, accum_out=sums[:, tt, 1, oc:oc + 1])
+            if oc < NSINGLE:
+                parked.append((oc, tt, hv))
 
-        def park():
-            while parked:
-                oc, tt, h = parked.pop(0)
-                nc.sync.dma_start(out=out[0, P * tt:P * (tt + 1), 256 * oc:256 * (oc + 1)], in_=h[:])
+        def park(keep):
+            while len(parked) > keep:
+                oc, tt, hv = parked.pop(0)
+                nc.sync.dma_start(out=out[0, P * tt:P * (tt + 1), 256 * oc:256 * (oc + 1)], in_=hv)
 
         def finalize(tt):
-            ha, hb = rows.pop(tt)
+            ha, hb = rows_a.pop(tt), rows.pop(tt)
             st4 = sb.tile([P, 4], F32, name="st4", tag="st4", bufs=2)
             rstd = sb.tile([P, 1], F32, name="rstd", tag="rstd", bufs=2)
             nc.vector.tensor_reduce(out=st4[:, 0:2], in_=sums[:, tt, :, :], axis=AX.X, op=ALU.add)
             nc.vector.tensor_scalar(out=st4[:, 2:3], in0=st4[:, 0:1], scalar1=st4[:, 0:1], scalar2=EPS, op0=ALU.mult, op1=ALU.subtract)
             nc.vector.tensor_tensor(out=st4[:, 3:4], in0=st4[:, 1:2], in1=st4[:, 2:3], op=ALU.subtract)
             nc.gpsimd.tensor_tensor(out=rstd[:], in0=st4[:, 3:4], in1=neg_half[:], op=ALU.pow)
-            for i, hx in enumerate((ha, hb)):
-                nc.vector.scalar_tensor_tensor(out=hx[:], in0=hx[:], scalar=st4[:, 0:1], in1=gb[("g", i)][:], op0=ALU.subtract, op1=ALU.mult)
-            for i, hx in enumerate((ha, hb)):
-                nc.vector.scalar_tensor_tensor(out=hx[:], in0=hx[:], scalar=rstd[:], in1=gb[("b", i)][:], op0=ALU.mult, op1=ALU.add)
+            for i, hx in ((1, hb), (0, ha)):
+                nc.vector.scalar_tensor_tensor(out=hx[:], in0=hx[:], scalar=st4[:, 0:1], in1=gb["g"][:, 1024 * i:1024 * (i + 1)], op0=ALU.subtract, op1=ALU.mult)
+            for i, hx in ((1, hb), (0, ha)):
+                nc.vector.scalar_tensor_tensor(out=hx[:], in0=hx[:], scalar=rstd[:], in1=gb["b"][:, 1024 * i:1024 * (i + 1)], op0=ALU.mult, op1=ALU.add)
                 nc.scalar.dma_start(out=out[0, P * tt:P * (tt + 1), 1024 * i:1024 * (i + 1)], in_=hx[:])
 
-        load_bo(0)
-        for j in range(3):
-            load_x(j)
-        add_bias(0)
+        load_x(x_pos[3])
+        add_bias(x_pos[1])
         to_finalize = []
         for j in range(len(jobs)):
             st = 66 + j
@@ -369,31 +437,29 @@ def tile_softmaxattention_pb_l_kernel(tc, attn, pz, Wo, bo, x, gamma, beta, out)
                 t_transpose(u)
             if any(("w", oc, gp) not in t_code for gp in range(8)):
                 t_quantize()
+            for u in sort_at[st]:
+                t_sort(u)
             if j == 0:
                 c_quantize(63)
-            if st == gb_step:
-                for i in range(2):
-                    for nm, src in (("g", gamma), ("b", beta)):
-                        t = sb.tile([P, 1024], BF16, name="gb", tag="code", bufs=NCODE, align_bytes=64)
-                        nc.sync.dma_start(out=t[:], in_=src[1024 * i:1024 * (i + 1)].partition_broadcast(P))
-                        gb[(nm, i)] = t
-            if j + 1 < len(jobs) and jobs[j + 1][0] not in bobs:
-                load_bo(jobs[j + 1][0])
-            if j + 2 < len(jobs) and jobs[j + 2][0] not in bobs:
-                load_bo(jobs[j + 2][0])
-            load_x(j + 3)
-            add_bias(j + 1)
+            if st == last_t_step + 1:
+                for nm, vec in (("g", gamma), ("b", beta)):
+                    t = sb.tile([P, D], BF16, name="gb", tag="srt", bufs=NSRT, align_bytes=64)
+                    nc.sync.dma_start(out=t[:], in_=vec.partition_broadcast(P))
+                    gb[nm] = t
             if j + 4 >= first_job[NSINGLE]:
                 raw_cap[0] = NRAW - 1
+            load_x(x_pos[j + 3] if j + 3 < n_single else len(xlist))
             if oc >= NSINGLE:
-                load_rows(tt + 1 if st > last_t_step else tt)
+                load_hb(tt + 2 if st > last_t_step else tt)
+                load_ha(tt + 1 if st > last_t_step else tt)
+            elif j + 2 >= first_job[NSINGLE]:
+                load_hb(0)
+            add_bias(x_pos[j + 2] if j + 2 < n_single else len(xlist))
             y_matmuls(j)
             if oc < NSINGLE:
-                if len(parked) > 1:
-                    oc0, tt0, h0 = parked.pop(0)
-                    nc.sync.dma_start(out=out[0, P * tt0:P * (tt0 + 1), 256 * oc0:256 * (oc0 + 1)], in_=h0[:])
+                park(1)
             else:
-                park()
+                park(0)
                 if oc == NSINGLE:
                     while to_finalize:
                         finalize(to_finalize.pop(0))

@@ -91,7 +91,7 @@ def tile_softmaxattention_pb_l_kernel(tc, attn, pz, Wo, bo, x, gamma, beta, out)
         live -= len([u for u in t_at[st] if u in presorted])
         for d in (1, 2):
             for u in t_at[min(st + d, NSTEP - 1)]:
-                if u not in presorted and u[0:2] != ("a", 0) and live < NSRT and st + d < NSTEP:
+                if u not in presorted and st + d >= 66 and live < NSRT and st + d < NSTEP:
                     sort_at[st].append(u)
                     presorted.add(u)
                     live += 1

@@ -27,6 +27,13 @@ NPLANE = 8
 NHALF = 9
 NF1K = 5
 NSRT = 2
+WIDE_TC = ()
+T3_ENG = "SV"
+PAIR_SLOTS = (3, 6, 7, 11, 15)
+SORT1 = 0
+SORT1_ENG = "V"
+SORT2_ENG = "VS"
+VEC_BANKS = ((), (), (), ())
 NSINGLE = 5
 NOC = 8
 NSTEP = 2 + 64 + 128
@@ -51,10 +58,8 @@ def tile_softmaxattention_pb_l_kernel(tc, attn, pz, Wo, bo, x, gamma, beta, out)
         for i, (tc_, g) in enumerate(units):
             if m == 0:
                 st = 1 + tc_
-            elif m == 1:
-                st = 2 + 3 + (i * 13) // 10
             else:
-                st = 2 + 16 * (m - 1) + (i * 16) // 10
+                st = 2 + 16 * (m - 1) + PAIR_SLOTS[i // 2]
             t_at[st].append(("a", m, tc_, g))
             for z in range(st, 2 + 16 * m + 12 + tc_ + 1):
                 mand[z] += 1
@@ -67,7 +72,7 @@ def tile_softmaxattention_pb_l_kernel(tc, attn, pz, Wo, bo, x, gamma, beta, out)
         end = 66 + last_job[oc]
         while True:
             if st < 66:
-                ok = len(t_at[st]) < 1 and ((st - 50) * 10) // 16 != ((st - 49) * 10) // 16
+                ok = len(t_at[st]) < 2 and (st - 50) in PAIR_SLOTS
             elif st < 66 + first_job[NSINGLE]:
                 ok = len(t_at[st]) < 2 and (st % 2 == 0)
             else:
@@ -84,6 +89,14 @@ def tile_softmaxattention_pb_l_kernel(tc, attn, pz, Wo, bo, x, gamma, beta, out)
 
     last_t_step = max(z for z in range(NSTEP) if t_at[z])
 
+    sort1 = set()
+    for m in range(H):
+        seen = 0
+        for st in range(2 + 16 * m + (3 if m == 0 else 0), 2 + 16 * (m + 1)):
+            for u in t_at[st]:
+                if (seen * SORT1) // 10 != ((seen + 1) * SORT1) // 10:
+                    sort1.add(u)
+                seen += 1
     sort_at = [[] for st in range(NSTEP)]
     presorted = set()
     live = 0
@@ -91,7 +104,7 @@ def tile_softmaxattention_pb_l_kernel(tc, attn, pz, Wo, bo, x, gamma, beta, out)
         live -= len([u for u in t_at[st] if u in presorted])
         for d in (1, 2):
             for u in t_at[min(st + d, NSTEP - 1)]:
-                if u not in presorted and st + d >= 66 and live < NSRT and st + d < NSTEP:
+                if u not in presorted and (st + d >= 66 or u in sort1) and live < NSRT and st + d < NSTEP:
                     sort_at[st].append(u)
                     presorted.add(u)
                     live += 1
@@ -137,10 +150,12 @@ def tile_softmaxattention_pb_l_kernel(tc, attn, pz, Wo, bo, x, gamma, beta, out)
 
         rows = {}
         rows_a = {}
+        c_flat = {}
+        reserve = [0]
         raw_cap = [NRAW]
 
         def issue_raw():
-            while issued[0] < len(raw_order) and len(raws) < raw_cap[0] and len(raws) + len(rows_a) + len([z for z in rows if z % 5 >= 3]) < NRAW:
+            while issued[0] < len(raw_order) and len(raws) < raw_cap[0] and len(raws) + len(c_flat) + reserve[0] + len(rows_a) + len([z for z in rows if z % 5 >= 3]) < NRAW:
                 issue_one_raw()
 
         def issue_one_raw():
@@ -169,6 +184,7 @@ def tile_softmaxattention_pb_l_kernel(tc, attn, pz, Wo, bo, x, gamma, beta, out)
 
         issue_raw()
 
+        in_stage1 = [True]
         t_code = {}
         t_plane = {}
         pending = []
@@ -193,7 +209,8 @@ def tile_softmaxattention_pb_l_kernel(tc, attn, pz, Wo, bo, x, gamma, beta, out)
             raw32 = raws.pop(u)[:].bitcast(F32)
             srt = sb.tile([P, 1024], F32, name="srt", tag="srt", bufs=NSRT, align_bytes=64)
             n_sorted[0] += 1
-            if u[0] == "w" or n_sorted[0] % 2 == 0:
+            which = SORT1_ENG if u in sort1 else SORT2_ENG
+            if which[n_sorted[0] % len(which)] == "V":
                 eng = nc.vector.tensor_copy
             else:
                 eng = nc.scalar.copy
@@ -230,7 +247,11 @@ def tile_softmaxattention_pb_l_kernel(tc, attn, pz, Wo, bo, x, gamma, beta, out)
             grp = new_grp()
             g32 = grp[:].bitcast(F32)
             for b in range(2):
-                nc.scalar.copy(
+                if T3_ENG[b] == "V" and in_stage1[0]:
+                    evac = nc.vector.tensor_copy
+                else:
+                    evac = nc.scalar.copy
+                evac(
                     out=g32[:, 512 * b:512 * (b + 1)].rearrange("p (c r w) -> p c r w", c=2, w=2),
                     in_=banks[b][:].rearrange("p (c w r) -> p c r w", c=2, w=2),
                 )
@@ -260,8 +281,40 @@ def tile_softmaxattention_pb_l_kernel(tc, attn, pz, Wo, bo, x, gamma, beta, out)
 
         c_grp = {}
 
+        def c_matmuls_wide(s):
+            m, ib, tc_ = s // 16, (s % 16) // 4, s % 4
+            flat = sb.tile([P, 2048], BF16, name="flat", tag="raw", bufs=NRAW, align_bytes=64)
+            c_flat[s] = flat
+            for t4 in range(4):
+                bank = new_bank()
+                for g in range(tc_ + 1):
+                    q = 16 * m + 4 * ib + g
+                    nc.tensor.matmul_mx(
+                        out=bank[:],
+                        lhsT=p_code[q][:, P * t4:P * (t4 + 1)].bitcast(FP8X4),
+                        lhsT_scale=p_plane[q][:, P * t4:P * (t4 + 1)],
+                        rhs=t_code[("a", m, tc_, g)][:].bitcast(FP8X4),
+                        rhs_scale=t_plane[("a", m, tc_)][4 * g:P, :],
+                        start=(g == 0),
+                        stop=(g == tc_),
+                    )
+                nc.scalar.copy(out=flat[:, 512 * t4:512 * (t4 + 1)], in_=bank[:])
+
+        def c_interleave(s):
+            if s in c_flat:
+                grp = new_grp()
+                nc.vector.tensor_copy(
+                    out=grp[:].rearrange("p (r j) -> p r j", j=4),
+                    in_=c_flat.pop(s)[:].rearrange("p (j r) -> p r j", j=4),
+                )
+                c_grp[s] = grp
+                issue_raw()
+
         def c_matmuls(s):
             m, ib, tc_ = s // 16, (s % 16) // 4, s % 4
+            if tc_ in WIDE_TC:
+                c_matmuls_wide(s)
+                return
             grp = new_grp()
             for tq in range(4):
                 bank = new_bank()
@@ -278,7 +331,11 @@ def tile_softmaxattention_pb_l_kernel(tc, attn, pz, Wo, bo, x, gamma, beta, out)
                             start=(g == 0),
                             stop=(g == tc_),
                         )
-                nc.scalar.copy(
+                if tq in VEC_BANKS[tc_]:
+                    evac = nc.vector.tensor_copy
+                else:
+                    evac = nc.scalar.copy
+                evac(
                     out=grp[:, 512 * tq:512 * (tq + 1)].rearrange("p (r j) -> p r j", j=4),
                     in_=bank[:].rearrange("p (j r) -> p r j", j=4),
                 )
@@ -301,8 +358,11 @@ def tile_softmaxattention_pb_l_kernel(tc, attn, pz, Wo, bo, x, gamma, beta, out)
             s = st - 2
             if 0 <= s + 1 < 64:
                 p_quantize(s + 1)
+            reserve[0] = 1 if ((s % 4) in WIDE_TC or ((s + 1) % 4) in WIDE_TC) and s >= 0 and s not in c_flat else 0
             if s + 2 < 64:
                 p_interleave(s + 2)
+            if s >= 1:
+                c_interleave(s - 1)
             t_quantize()
             for u in t_at[st]:
                 t_transpose(u)
@@ -426,6 +486,7 @@ def tile_softmaxattention_pb_l_kernel(tc, attn, pz, Wo, bo, x, gamma, beta, out)
                 nc.vector.scalar_tensor_tensor(out=hx[:], in0=hx[:], scalar=rstd[:], in1=gb["b"][:, 1024 * i:1024 * (i + 1)], op0=ALU.mult, op1=ALU.add)
                 nc.scalar.dma_start(out=out[0, P * tt:P * (tt + 1), 1024 * i:1024 * (i + 1)], in_=hx[:])
 
+        in_stage1[0] = False
         load_x(x_pos[3])
         add_bias(x_pos[1])
         to_finalize = []
@@ -440,6 +501,7 @@ def tile_softmaxattention_pb_l_kernel(tc, attn, pz, Wo, bo, x, gamma, beta, out)
             for u in sort_at[st]:
                 t_sort(u)
             if j == 0:
+                c_interleave(63)
                 c_quantize(63)
             if st == last_t_step + 1:
                 for nm, vec in (("g", gamma), ("b", beta)):

@@ -27,13 +27,6 @@ NPLANE = 8
 NHALF = 9
 NF1K = 5
 NSRT = 2
-WIDE_TC = ()
-T3_ENG = "SV"
-PAIR_SLOTS = (3, 6, 7, 11, 15)
-SORT1 = 0
-SORT1_ENG = "V"
-SORT2_ENG = "VS"
-VEC_BANKS = ((), (), (), ())
 NSINGLE = 5
 NOC = 8
 NSTEP = 2 + 64 + 128
@@ -58,8 +51,10 @@ def tile_softmaxattention_pb_l_kernel(tc, attn, pz, Wo, bo, x, gamma, beta, out)
         for i, (tc_, g) in enumerate(units):
             if m == 0:
                 st = 1 + tc_
+            elif m == 1:
+                st = 2 + 3 + (i * 13) // 10
             else:
-                st = 2 + 16 * (m - 1) + PAIR_SLOTS[i // 2]
+                st = 2 + 16 * (m - 1) + (i * 16) // 10
             t_at[st].append(("a", m, tc_, g))
             for z in range(st, 2 + 16 * m + 12 + tc_ + 1):
                 mand[z] += 1
@@ -72,7 +67,7 @@ def tile_softmaxattention_pb_l_kernel(tc, attn, pz, Wo, bo, x, gamma, beta, out)
         end = 66 + last_job[oc]
         while True:
             if st < 66:
-                ok = len(t_at[st]) < 2 and (st - 50) in PAIR_SLOTS
+                ok = len(t_at[st]) < 1 and ((st - 50) * 10) // 16 != ((st - 49) * 10) // 16
             elif st < 66 + first_job[NSINGLE]:
                 ok = len(t_at[st]) < 2 and (st % 2 == 0)
             else:
@@ -89,14 +84,6 @@ def tile_softmaxattention_pb_l_kernel(tc, attn, pz, Wo, bo, x, gamma, beta, out)
 
     last_t_step = max(z for z in range(NSTEP) if t_at[z])
 
-    sort1 = set()
-    for m in range(H):
-        seen = 0
-        for st in range(2 + 16 * m + (3 if m == 0 else 0), 2 + 16 * (m + 1)):
-            for u in t_at[st]:
-                if (seen * SORT1) // 10 != ((seen + 1) * SORT1) // 10:
-                    sort1.add(u)
-                seen += 1
     sort_at = [[] for st in range(NSTEP)]
     presorted = set()
     live = 0
@@ -104,7 +91,7 @@ def tile_softmaxattention_pb_l_kernel(tc, attn, pz, Wo, bo, x, gamma, beta, out)
         live -= len([u for u in t_at[st] if u in presorted])
         for d in (1, 2):
             for u in t_at[min(st + d, NSTEP - 1)]:
-                if u not in presorted and (st + d >= 66 or u in sort1) and live < NSRT and st + d < NSTEP:
+                if u not in presorted and st + d >= 66 and live < NSRT and st + d < NSTEP:
                     sort_at[st].append(u)
                     presorted.add(u)
                     live += 1
@@ -150,12 +137,10 @@ def tile_softmaxattention_pb_l_kernel(tc, attn, pz, Wo, bo, x, gamma, beta, out)
 
         rows = {}
         rows_a = {}
-        c_flat = {}
-        reserve = [0]
         raw_cap = [NRAW]
 
         def issue_raw():
-            while issued[0] < len(raw_order) and len(raws) < raw_cap[0] and len(raws) + len(c_flat) + reserve[0] + len(rows_a) + len([z for z in rows if z % 5 >= 3]) < NRAW:
+            while issued[0] < len(raw_order) and len(raws) < raw_cap[0] and len(raws) + len(rows_a) + len([z for z in rows if z % 5 >= 3]) < NRAW:
                 issue_one_raw()
 
         def issue_one_raw():
@@ -184,7 +169,6 @@ def tile_softmaxattention_pb_l_kernel(tc, attn, pz, Wo, bo, x, gamma, beta, out)
 
         issue_raw()
 
-        in_stage1 = [True]
         t_code = {}
         t_plane = {}
         pending = []
@@ -209,8 +193,7 @@ def tile_softmaxattention_pb_l_kernel(tc, attn, pz, Wo, bo, x, gamma, beta, out)
             raw32 = raws.pop(u)[:].bitcast(F32)
             srt = sb.tile([P, 1024], F32, name="srt", tag="srt", bufs=NSRT, align_bytes=64)
             n_sorted[0] += 1
-            which = SORT1_ENG if u in sort1 else SORT2_ENG
-            if which[n_sorted[0] % len(which)] == "V":
+            if u[0] == "w" or n_sorted[0] % 2 == 0:
                 eng = nc.vector.tensor_copy
             else:
                 eng = nc.scalar.copy
@@ -247,11 +230,7 @@ def tile_softmaxattention_pb_l_kernel(tc, attn, pz, Wo, bo, x, gamma, beta, out)
             grp = new_grp()
             g32 = grp[:].bitcast(F32)
             for b in range(2):
-                if T3_ENG[b] == "V" and in_stage1[0]:
-                    evac = nc.vector.tensor_copy
-                else:
-                    evac = nc.scalar.copy
-                evac(
+                nc.scalar.copy(
                     out=g32[:, 512 * b:512 * (b + 1)].rearrange("p (c r w) -> p c r w", c=2, w=2),
                     in_=banks[b][:].rearrange("p (c w r) -> p c r w", c=2, w=2),
                 )
@@ -266,8 +245,8 @@ def tile_softmaxattention_pb_l_kernel(tc, attn, pz, Wo, bo, x, gamma, beta, out)
             raw = raws.pop(u)
             grp = new_grp()
             nc.vector.tensor_copy(
-                out=grp[:].rearrange("p (t m j) -> p t m j", t=4, j=4),
-                in_=raw[:].rearrange("p (j m t) -> p t m j", j=4, t=4),
+                out=grp[:].rearrange("p (t m j) -> p m t j", t=4, j=4),
+                in_=raw[:].rearrange("p (j m t) -> p m t j", j=4, t=4),
             )
             issue_raw()
             p_grp[q] = grp
@@ -281,40 +260,8 @@ def tile_softmaxattention_pb_l_kernel(tc, attn, pz, Wo, bo, x, gamma, beta, out)
 
         c_grp = {}
 
-        def c_matmuls_wide(s):
-            m, ib, tc_ = s // 16, (s % 16) // 4, s % 4
-            flat = sb.tile([P, 2048], BF16, name="flat", tag="raw", bufs=NRAW, align_bytes=64)
-            c_flat[s] = flat
-            for t4 in range(4):
-                bank = new_bank()
-                for g in range(tc_ + 1):
-                    q = 16 * m + 4 * ib + g
-                    nc.tensor.matmul_mx(
-                        out=bank[:],
-                        lhsT=p_code[q][:, P * t4:P * (t4 + 1)].bitcast(FP8X4),
-                        lhsT_scale=p_plane[q][:, P * t4:P * (t4 + 1)],
-                        rhs=t_code[("a", m, tc_, g)][:].bitcast(FP8X4),
-                        rhs_scale=t_plane[("a", m, tc_)][4 * g:P, :],
-                        start=(g == 0),
-                        stop=(g == tc_),
-                    )
-                nc.scalar.copy(out=flat[:, 512 * t4:512 * (t4 + 1)], in_=bank[:])
-
-        def c_interleave(s):
-            if s in c_flat:
-                grp = new_grp()
-                nc.vector.tensor_copy(
-                    out=grp[:].rearrange("p (r j) -> p r j", j=4),
-                    in_=c_flat.pop(s)[:].rearrange("p (j r) -> p r j", j=4),
-                )
-                c_grp[s] = grp
-                issue_raw()
-
         def c_matmuls(s):
             m, ib, tc_ = s // 16, (s % 16) // 4, s % 4
-            if tc_ in WIDE_TC:
-                c_matmuls_wide(s)
-                return
             grp = new_grp()
             for tq in range(4):
                 bank = new_bank()
@@ -331,11 +278,7 @@ def tile_softmaxattention_pb_l_kernel(tc, attn, pz, Wo, bo, x, gamma, beta, out)
                             start=(g == 0),
                             stop=(g == tc_),
                         )
-                if tq in VEC_BANKS[tc_]:
-                    evac = nc.vector.tensor_copy
-                else:
-                    evac = nc.scalar.copy
-                evac(
+                nc.scalar.copy(
                     out=grp[:, 512 * tq:512 * (tq + 1)].rearrange("p (r j) -> p r j", j=4),
                     in_=bank[:].rearrange("p (j r) -> p r j", j=4),
                 )
@@ -358,11 +301,8 @@ def tile_softmaxattention_pb_l_kernel(tc, attn, pz, Wo, bo, x, gamma, beta, out)
             s = st - 2
             if 0 <= s + 1 < 64:
                 p_quantize(s + 1)
-            reserve[0] = 1 if ((s % 4) in WIDE_TC or ((s + 1) % 4) in WIDE_TC) and s >= 0 and s not in c_flat else 0
             if s + 2 < 64:
                 p_interleave(s + 2)
-            if s >= 1:
-                c_interleave(s - 1)
             t_quantize()
             for u in t_at[st]:
                 t_transpose(u)
@@ -486,7 +426,6 @@ def tile_softmaxattention_pb_l_kernel(tc, attn, pz, Wo, bo, x, gamma, beta, out)
                 nc.vector.scalar_tensor_tensor(out=hx[:], in0=hx[:], scalar=rstd[:], in1=gb["b"][:, 1024 * i:1024 * (i + 1)], op0=ALU.mult, op1=ALU.add)
                 nc.scalar.dma_start(out=out[0, P * tt:P * (tt + 1), 1024 * i:1024 * (i + 1)], in_=hx[:])
 
-        in_stage1[0] = False
         load_x(x_pos[3])
         add_bias(x_pos[1])
         to_finalize = []
@@ -501,7 +440,6 @@ def tile_softmaxattention_pb_l_kernel(tc, attn, pz, Wo, bo, x, gamma, beta, out)
             for u in sort_at[st]:
                 t_sort(u)
             if j == 0:
-                c_interleave(63)
                 c_quantize(63)
             if st == last_t_step + 1:
                 for nm, vec in (("g", gamma), ("b", beta)):

from contextlib import ExitStack

import concourse.mybir as mybir
from concourse.masks import make_identity

F32 = mybir.dt.float32
BF16 = mybir.dt.bfloat16
U32 = mybir.dt.uint32
U8 = mybir.dt.uint8
FP8X4 = mybir.dt.float8_e4m3fn_x4
ALU = mybir.AluOpType
ACT = mybir.ActivationFunctionType
AX = mybir.AxisListType

P = 128
T = 2048
D = 2048
H = 4
MD = H * D
EPS = 1e-5
FLOPS = 2 * H * D * (1024 * 1024 + 1024 * 2048) + 2 * T * MD * D

NCODE = 25
NRAW = 4
NGRP = 3
NPLANE = 8
NHALF = 9
NF1K = 5
NSRT = 2
NSINGLE = 5
NOC = 8
NSTEP = 2 + 64 + 128


def tile_softmaxattention_pb_l_kernel(tc, attn, pz, Wo, bo, x, gamma, beta, out):
    nc = tc.nc

    jobs = [(oc, tt) for oc in range(NSINGLE) for tt in range(16)]
    jobs += [(oc, tt) for tt in range(16) for oc in range(NSINGLE, NOC)]
    first_job = {}
    last_job = {}
    for j, (oc, tt) in enumerate(jobs):
        if oc not in first_job:
            first_job[oc] = j
        last_job[oc] = j

    t_at = [[] for st in range(NSTEP)]
    mand = [0] * NSTEP
    for m in range(H):
        units = [(tc_, g) for tc_ in range(4) for g in range(tc_ + 1)]
        for i, (tc_, g) in enumerate(units):
            if m == 0:
                st = 1 + tc_
            elif m == 1:
                st = 2 + 3 + (i * 13) // 10
            else:
                st = 2 + 16 * (m - 1) + (i * 16) // 10
            t_at[st].append(("a", m, tc_, g))
            for z in range(st, 2 + 16 * m + 12 + tc_ + 1):
                mand[z] += 1
    for q in range(64):
        for z in range(q + 1, 2 + 4 * (q // 4) + 3 + 1):
            mand[z] += 1
    st = 2 + 48
    for w in range(NOC * 8):
        oc = w // 8
        end = 66 + last_job[oc]
        while True:
            if st < 66:
                ok = len(t_at[st]) < 1 and ((st - 50) * 10) // 16 != ((st - 49) * 10) // 16
            elif st < 66 + first_job[NSINGLE]:
                ok = len(t_at[st]) < 2 and (st % 2 == 0)
            else:
                ok = len(t_at[st]) < 3
            if ok:
                ok = all(mand[z] + 1 <= NCODE for z in range(st, end + 1))
            if ok:
                break
            st += 1
        assert st <= 66 + first_job[oc], "a Wo unit comes too late"
        t_at[st].append(("w", oc, w % 8))
        for z in range(st, end + 1):
            mand[z] += 1

    last_t_step = max(z for z in range(NSTEP) if t_at[z])

    sort_at = [[] for st in range(NSTEP)]
    presorted = set()
    live = 0
    for st in range(NSTEP):
        live -= len([u for u in t_at[st] if u in presorted])
        for d in (1, 2):
            for u in t_at[min(st + d, NSTEP - 1)]:
                if u not in presorted and st + d >= 66 and live < NSRT and st + d < NSTEP:
                    sort_at[st].append(u)
                    presorted.add(u)
                    live += 1

    raw_order = []
    for st in range(NSTEP):
        q = st
        if q < 64:
            raw_order.append(("p", q // 16, (q % 16) // 4, q % 4))
        raw_order.extend(u for u in t_at[st] if u not in presorted)
        raw_order.extend(sort_at[st])

    with ExitStack() as ctx:
        ctx.enter_context(tc.manual_schedule())
        sb = ctx.enter_context(tc.tile_pool(name="sb", bufs=1))
        ps = ctx.enter_context(tc.psum_pool(name="ps", bufs=8))

        ident = sb.tile([P, P], F32, name="ident")
        make_identity(nc, ident[:])
        neg_half = sb.tile([P, 1], F32, name="neg_half")
        nc.vector.memset(neg_half[:], -0.5)
        warm = sb.tile([P, 1], F32, name="warm")
        nc.scalar.activation(out=warm[:], in_=neg_half[:], func=ACT.Square)
        sums = sb.tile([P, 16, 2, NOC], F32, name="sums")

        cat_code = [sb.tile([P, T], U32, name="cat%d" % g, align_bytes=64) for g in range(16)]
        cat_plane = [sb.tile([P, T], U8, name="catp%d" % i, align_bytes=64) for i in range(4)]

        def new_code():
            return sb.tile([P, 512], U32, name="code", tag="code", bufs=NCODE, align_bytes=64)

        def new_plane():
            return sb.tile([P, 512], U8, name="plane", tag="plane", bufs=NPLANE, align_bytes=64)

        def new_grp():
            return sb.tile([P, 2048], BF16, name="grp", tag="grp", bufs=NGRP, align_bytes=64)

        def new_bank():
            return ps.tile([P, 512], F32, name="bank", tag="bank")

        raws = {}
        issued = [0]

        rows = {}
        rows_a = {}
        raw_cap = [NRAW]

        def issue_raw():
            while issued[0] < len(raw_order) and len(raws) < raw_cap[0] and len(raws) + len(rows_a) + len([z for z in rows if z % 5 >= 3]) < NRAW:
                issue_one_raw()

        def issue_one_raw():
            u = raw_order[issued[0]]
            issued[0] += 1
            raw = sb.tile([P, 2048], BF16, name="raw", tag="raw", bufs=NRAW, align_bytes=64)
            if u[0] == "p":
                m, ib, g = u[1], u[2], u[3]
                nc.sync.dma_start(
                    out=raw[:].rearrange("p (j c) -> p j c", j=4),
                    in_=pz[0, m, 512 * g:512 * (g + 1), 512 * ib:512 * (ib + 1)].rearrange("(p j) c -> p j c", j=4),
                )
            elif u[0] == "a":
                m, tc_, g = u[1], u[2], u[3]
                nc.sync.dma_start(
                    out=raw[:].rearrange("p (a k) -> p a k", a=4),
                    in_=attn[0, m, 512 * tc_:512 * (tc_ + 1), 512 * g:512 * (g + 1)].rearrange("(a p) k -> p a k", p=P),
                )
            else:
                oc, gp = u[1], u[2]
                nc.sync.dma_start(
                    out=raw[:].rearrange("p (a k) -> p a k", a=2),
                    in_=Wo[256 * oc:256 * (oc + 1), 1024 * gp:1024 * (gp + 1)].rearrange("(a p) k -> p a k", p=P),
                )
            raws[u] = raw

        issue_raw()

        t_code = {}
        t_plane = {}
        pending = []

        def t_quantize():
            while pending:
                u, grp = pending.pop(0)
                if u[0] == "a":
                    pkey, k = ("a", u[1], u[2]), 4 * u[3]
                else:
                    pkey, k = ("w", u[1], u[2] // 4), 4 * (u[2] % 4)
                if pkey not in t_plane:
                    t_plane[pkey] = new_plane()
                code = new_code()
                nc.vector.quantize_mx(out=code[:].bitcast(FP8X4), scales=t_plane[pkey][k:P, :], in_=grp[:])
                t_code[u] = code

        sorted_words = {}
        n_sorted = [0]

        def t_sort(u):
            raw32 = raws.pop(u)[:].bitcast(F32)
            srt = sb.tile([P, 1024], F32, name="srt", tag="srt", bufs=NSRT, align_bytes=64)
            n_sorted[0] += 1
            if u[0] == "w" or n_sorted[0] % 2 == 0:
                eng = nc.vector.tensor_copy
            else:
                eng = nc.scalar.copy
            eng(
                out=srt[:].rearrange("p (c w k) -> p c w k", c=4, w=2),
                in_=raw32.rearrange("p (c k w) -> p c w k", c=4, w=2),
            )
            issue_raw()
            sorted_words[u] = srt

        def t_transpose(u):
            if u in sorted_words:
                words, step = sorted_words.pop(u), 1
            else:
                words, step = raws.pop(u)[:].bitcast(F32), 2
            if u[0] == "a":
                bases = [0, 256, 512, 768]
            else:
                bases = [0, 512, 256, 768]
            banks = []
            for b in range(2):
                bank = new_bank()
                for c in range(2):
                    base = bases[2 * b + c]
                    for w in range(2):
                        col = (2 * c + w) * P
                        if step == 1:
                            nc.tensor.transpose(bank[:, col:col + P], words[:, base + P * w:base + P * (w + 1)], ident[:])
                        else:
                            nc.tensor.transpose(bank[:, col:col + P], words[:, base + w:base + 256:2], ident[:])
                banks.append(bank)
            issue_raw()
            t_quantize()
            grp = new_grp()
            g32 = grp[:].bitcast(F32)
            for b in range(2):
                nc.scalar.copy(
                    out=g32[:, 512 * b:512 * (b + 1)].rearrange("p (c r w) -> p c r w", c=2, w=2),
                    in_=banks[b][:].rearrange("p (c w r) -> p c r w", c=2, w=2),
                )
            pending.append((u, grp))

        p_grp = {}
        p_code = {}
        p_plane = {}

        def p_interleave(q):
            u = ("p", q // 16, (q % 16) // 4, q % 4)
            raw = raws.pop(u)
            grp = new_grp()
            nc.vector.tensor_copy(
                out=grp[:].rearrange("p (t m j) -> p m t j", t=4, j=4),
                in_=raw[:].rearrange("p (j m t) -> p m t j", j=4, t=4),
            )
            issue_raw()
            p_grp[q] = grp

        def p_quantize(q):
            code = new_code()
            plane = sb.tile([P, 512], U8, name="pplane", tag="half", bufs=NHALF, align_bytes=64)
            nc.vector.quantize_mx(out=code[:].bitcast(FP8X4), scales=plane[:], in_=p_grp.pop(q)[:])
            p_code[q] = code
            p_plane[q] = plane

        c_grp = {}

        def c_matmuls(s):
            m, ib, tc_ = s // 16, (s % 16) // 4, s % 4
            grp = new_grp()
            for tq in range(4):
                bank = new_bank()
                for t4 in range(4):
                    for g in range(tc_ + 1):
                        q = 16 * m + 4 * ib + g
                        a = ("a", m, tc_, g)
                        nc.tensor.matmul_mx(
                            out=bank[:, P * t4:P * (t4 + 1)],
                            lhsT=p_code[q][:, P * t4:P * (t4 + 1)].bitcast(FP8X4),
                            lhsT_scale=p_plane[q][:, P * t4:P * (t4 + 1)],
                            rhs=t_code[a][:, P * tq:P * (tq + 1)].bitcast(FP8X4),
                            rhs_scale=t_plane[("a", m, tc_)][4 * g:P, P * tq:P * (tq + 1)],
                            start=(g == 0),
                            stop=(g == tc_),
                        )
                nc.scalar.copy(
                    out=grp[:, 512 * tq:512 * (tq + 1)].rearrange("p (r j) -> p r j", j=4),
                    in_=bank[:].rearrange("p (j r) -> p r j", j=4),
                )
            c_grp[s] = grp

        def cat_slot(g):
            return cat_plane[(g // 8) * 2 + g % 2], 4 * ((g // 2) % 4)

        def c_quantize(s):
            m, ib, tc_ = s // 16, (s % 16) // 4, s % 4
            g = 4 * m + ib
            plane, k = cat_slot(g)
            nc.vector.quantize_mx(
                out=cat_code[g][:, 512 * tc_:512 * (tc_ + 1)].bitcast(FP8X4),
                scales=plane[k:P, 512 * tc_:512 * (tc_ + 1)],
                in_=c_grp.pop(s)[:],
            )

        for st in range(66):
            s = st - 2
            if 0 <= s + 1 < 64:
                p_quantize(s + 1)
            if s + 2 < 64:
                p_interleave(s + 2)
            t_quantize()
            for u in t_at[st]:
                t_transpose(u)
            for u in sort_at[st]:
                t_sort(u)
            if s >= 1:
                c_quantize(s - 1)
            if s >= 0:
                c_matmuls(s)

        xts = {}
        hdst = {}
        bobs = {}
        gb = {}
        parked = []
        next_rows = [0]
        next_a = [0]
        next_x = [0]
        next_bias = [0]
        junk = sb.tile([P, 256], BF16, name="junk", align_bytes=64)

        n_single = 16 * NSINGLE
        late = [(oc, tt) for tt in range(16) for oc in range(NSINGLE, NOC)]
        xlist = []
        x_pos = {}
        for j in range(n_single):
            x_pos[j] = len(xlist)
            xlist.append((jobs[j][0], jobs[j][1], j))
            for i in range((j * len(late)) // (n_single - 8), min(len(late), ((j + 1) * len(late)) // (n_single - 8))):
                xlist.append((late[i][0], late[i][1], -1))

        def load_x(upto):
            while next_x[0] <= min(upto, len(xlist) - 1):
                j = next_x[0]
                next_x[0] += 1
                oc, tt = xlist[j][0], xlist[j][1]
                if oc not in bobs:
                    bob = sb.tile([P, 256], BF16, name="bob", tag="half", bufs=NHALF, align_bytes=64)
                    nc.sync.dma_start(out=bob[:], in_=bo[256 * oc:256 * (oc + 1)].partition_broadcast(P))
                    bobs[oc] = bob
                xt = sb.tile([P, 256], BF16, name="xt", tag="half", bufs=NHALF, align_bytes=64)
                nc.sync.dma_start(out=xt[:], in_=x[0, P * tt:P * (tt + 1), 256 * oc:256 * (oc + 1)])
                xts[j] = xt

        def load_hb(upto):
            while next_rows[0] <= min(upto, 15):
                tt = next_rows[0]
                if tt % 5 < 3:
                    if len(pending) + len([z for z in rows if z % 5 < 3]) >= NGRP:
                        return
                    hb = sb.tile([P, 1024], F32, name="hb", tag="grp", bufs=NGRP, align_bytes=64)
                else:
                    if len(raws) + len(rows_a) + len([z for z in rows if z % 5 >= 3]) >= NRAW:
                        return
                    hb = sb.tile([P, 1024], F32, name="hb", tag="raw", bufs=NRAW, align_bytes=64)
                next_rows[0] += 1
                nc.sync.dma_start(out=hb[:], in_=out[0, P * tt:P * (tt + 1), 1024:2048])
                rows[tt] = hb

        def load_ha(upto):
            while next_a[0] <= min(upto, 15) and len(rows_a) < 2 and len(raws) + len(rows_a) + len([z for z in rows if z % 5 >= 3]) < NRAW:
                tt = next_a[0]
                next_a[0] += 1
                ha = sb.tile([P, 1024], F32, name="ha", tag="raw", bufs=NRAW, align_bytes=64)
                nc.sync.dma_start(out=ha[:], in_=out[0, P * tt:P * (tt + 1), 0:1024])
                rows_a[tt] = ha

        def add_bias(upto):
            while next_bias[0] <= min(upto, len(xlist) - 1):
                i = next_bias[0]
                next_bias[0] += 1
                oc, tt, j = xlist[i]
                h = sb.tile([P, 256], F32, name="h", tag="f1k", bufs=NF1K, align_bytes=64)
                nc.gpsimd.tensor_tensor(out=h[:], in0=xts.pop(i)[:], in1=bobs[oc][:], op=ALU.add)
                if j >= 0:
                    hdst[j] = h[:]
                else:
                    parked.append((oc, tt, h[:]))

        def y_matmuls(j):
            oc, tt = jobs[j]
            bank = new_bank()
            for g in range(16):
                gp, gg = g // 2, g % 2
                plane, k = cat_slot(g)
                nc.tensor.matmul_mx(
                    out=bank[:, 0:256],
                    lhsT=cat_code[g][:, P * tt:P * (tt + 1)].bitcast(FP8X4),
                    lhsT_scale=plane[k:P, P * tt:P * (tt + 1)],
                    rhs=t_code[("w", oc, gp)][:, 256 * gg:256 * (gg + 1)].bitcast(FP8X4),
                    rhs_scale=t_plane[("w", oc, gp // 4)][k:P, 256 * gg:256 * (gg + 1)],
                    start=(g == 0),
                    stop=(g == 15),
                )
            if oc < NSINGLE:
                hv = hdst.pop(j)
            else:
                hv = rows[tt][:, 256 * (oc - 4):256 * (oc - 3)]
            nc.vector.tensor_tensor(out=hv, in0=bank[:, 0:256], in1=hv, op=ALU.add)
            nc.scalar.activation(out=junk[:], in_=hv, func=ACT.Identity, scale=1.0 / D, accum_out=sums[:, tt, 0, oc:oc + 1])
            nc.scalar.activation(out=junk[:], in_=hv, func=ACT.Square, scale=D ** -0.5, accum_out=sums[:, tt, 1, oc:oc + 1])
            if oc < NSINGLE:
                parked.append((oc, tt, hv))

        def park(keep):
            while len(parked) > keep:
                oc, tt, hv = parked.pop(0)
                nc.sync.dma_start(out=out[0, P * tt:P * (tt + 1), 256 * oc:256 * (oc + 1)], in_=hv)

        def finalize(tt):
            ha, hb = rows_a.pop(tt), rows.pop(tt)
            st4 = sb.tile([P, 4], F32, name="st4", tag="st4", bufs=2)
            rstd = sb.tile([P, 1], F32, name="rstd", tag="rstd", bufs=2)
            nc.vector.tensor_reduce(out=st4[:, 0:2], in_=sums[:, tt, :, :], axis=AX.X, op=ALU.add)
            nc.vector.tensor_scalar(out=st4[:, 2:3], in0=st4[:, 0:1], scalar1=st4[:, 0:1], scalar2=EPS, op0=ALU.mult, op1=ALU.subtract)
            nc.vector.tensor_tensor(out=st4[:, 3:4], in0=st4[:, 1:2], in1=st4[:, 2:3], op=ALU.subtract)
            nc.gpsimd.tensor_tensor(out=rstd[:], in0=st4[:, 3:4], in1=neg_half[:], op=ALU.pow)
            for i, hx in ((1, hb), (0, ha)):
                nc.vector.scalar_tensor_tensor(out=hx[:], in0=hx[:], scalar=st4[:, 0:1], in1=gb["g"][:, 1024 * i:1024 * (i + 1)], op0=ALU.subtract, op1=ALU.mult)
            for i, hx in ((1, hb), (0, ha)):
                nc.vector.scalar_tensor_tensor(out=hx[:], in0=hx[:], scalar=rstd[:], in1=gb["b"][:, 1024 * i:1024 * (i + 1)], op0=ALU.mult, op1=ALU.add)
                nc.scalar.dma_start(out=out[0, P * tt:P * (tt + 1), 1024 * i:1024 * (i + 1)], in_=hx[:])

        load_x(x_pos[3])
        add_bias(x_pos[1])
        to_finalize = []
        for j in range(len(jobs)):
            st = 66 + j
            oc, tt = jobs[j]
            t_quantize()
            for u in t_at[st]:
                t_transpose(u)
            if any(("w", oc, gp) not in t_code for gp in range(8)):
                t_quantize()
            for u in sort_at[st]:
                t_sort(u)
            if j == 0:
                c_quantize(63)
            if st == last_t_step + 1:
                for nm, vec in (("g", gamma), ("b", beta)):
                    t = sb.tile([P, D], BF16, name="gb", tag="srt", bufs=NSRT, align_bytes=64)
                    nc.sync.dma_start(out=t[:], in_=vec.partition_broadcast(P))
                    gb[nm] = t
            if j + 4 >= first_job[NSINGLE]:
                raw_cap[0] = NRAW - 1
            load_x(x_pos[j + 3] if j + 3 < n_single else len(xlist))
            if oc >= NSINGLE:
                load_hb(tt + 2 if st > last_t_step else tt)
                load_ha(tt + 1 if st > last_t_step else tt)
            elif j + 2 >= first_job[NSINGLE]:
                load_hb(0)
            add_bias(x_pos[j + 2] if j + 2 < n_single else len(xlist))
            y_matmuls(j)
            if oc < NSINGLE:
                park(1)
            else:
                park(0)
                if oc == NSINGLE:
                    while to_finalize:
                        finalize(to_finalize.pop(0))
                if oc == NOC - 1:
                    to_finalize.append(tt)
        while to_finalize:
            finalize(to_finalize.pop(0))
